import numpy as np
import ml_dtypes


def mxq(x, axis, fmt="e4m3"):
    dtype, down = {"e4m3": (ml_dtypes.float8_e4m3fn, 7), "e5m2": (ml_dtypes.float8_e5m2, 14)}[fmt]
    v = np.moveaxis(np.asarray(x, np.float32).astype(ml_dtypes.bfloat16).astype(np.float64), axis, -1)
    blocks = v.reshape(v.shape[:-1] + (-1, 32))
    amax = np.abs(blocks).max(-1, keepdims=True)
    byte = np.maximum(np.where(amax > 0, np.frexp(amax)[1] - 1 + 127, 0) - down, 1)
    scale = np.exp2(byte - 127.0)
    codes = (blocks / scale).astype(np.float32).astype(dtype).astype(np.float64)
    return np.moveaxis((codes * scale).reshape(v.shape), -1, axis)


WIDE = False


def mx_kscale(k):
    if not WIDE:
        return np.ones(k)
    levels = np.array([10, -10, 5, -5, 0])
    a = np.random.permutation(np.resize(levels, k // 512 * 4)).reshape(k // 512, 4)
    idx = np.arange(k)
    return np.exp2(a[idx // 512, idx % 128 // 32])


BF16 = ml_dtypes.bfloat16


def bf(x):
    return np.asarray(x, np.float32).astype(BF16)


def f64(x):
    return np.asarray(x).astype(np.float64)


E2M1 = np.array([0.0, 0.5, 1.0, 1.5, 2.0, 3.0, 4.0, 6.0, -0.0, -0.5, -1.0, -1.5, -2.0, -3.0, -4.0, -6.0])


def pack_weight(w, fmt):
    k, n = w.shape
    w = f64(bf(w)).reshape(k // 32, 32, n)
    amax = np.abs(w).max(1)
    if fmt == "e4m3":
        byte = np.frexp(amax)[1] - 1 + 127 - 7
    else:
        mant, ex = np.frexp(amax / 6.0)
        byte = np.where(mant > 0.5, ex, ex - 1) + 127
    byte = np.clip(np.where(amax > 0, byte, 1), 1, 254)
    scaled = (w * np.exp2(127.0 - byte)[:, None, :]).reshape(k, n).astype(np.float32)
    by_word = np.ascontiguousarray(scaled.reshape(k // 512, 128, 4, n).transpose(0, 1, 3, 2))
    if fmt == "e4m3":
        words = by_word.astype(ml_dtypes.float8_e4m3fn).view(np.uint8)
    else:
        c = by_word.astype(ml_dtypes.float4_e2m1fn).view(np.uint8) & 0xF
        words = c[..., 0::2] | (c[..., 1::2] << 4)
    return np.ascontiguousarray(words), np.ascontiguousarray(byte.astype(np.uint8).reshape(k // 512, 16, n))


def unpack_weight(words, scales, fmt):
    g, p, n, _ = words.shape
    if fmt == "e4m3":
        vals = np.ascontiguousarray(words).view(ml_dtypes.float8_e4m3fn).astype(np.float64)
    else:
        nib = np.empty((g, p, n, 4), np.uint8)
        nib[..., 0::2] = words & 0xF
        nib[..., 1::2] = words >> 4
        vals = E2M1[nib]
    vals = vals * np.repeat(np.exp2(scales.astype(np.float64) - 127.0), 8, axis=1)[..., None]
    return vals.transpose(0, 1, 3, 2).reshape(g * 512, n)

def pack4(w):
    words, scales = pack_weight(w, "e2m1")
    return words.reshape(words.shape[0], 128, -1), scales


def unpack4(words, scales):
    return unpack_weight(words.reshape(words.shape[0], 128, -1, 2), scales, "e2m1")


T, D, F, R = 8192, 128, 512, 128


def setup_inputs():
    s = mx_kscale(F)
    h = bf(np.random.standard_normal((T, F)) * 0.75 * s)
    ha = bf(np.random.standard_normal((T, R)) * 0.75)
    words, scales = pack4(np.random.standard_normal((F, D)) / np.sqrt(F) / s[:, None])
    B_down = bf(np.random.standard_normal((R, D)) * 0.5 / np.sqrt(R))
    return {
        "h": h,
        "ha": ha,
        "W_down_words": words,
        "W_down_scales": scales,
        "B_down": B_down,
    }


def reference(h, ha, W_down_words, W_down_scales, B_down):
    return (mxq(f64(h), 1, "e4m3") @ unpack4(W_down_words, W_down_scales)) + f64(ha) @ f64(B_down)

@@ -1,0 +1,149 @@
+from contextlib import ExitStack
+
+import concourse.mybir as mybir
+from concourse.masks import make_identity
+
+F32 = mybir.dt.float32
+BF16 = mybir.dt.bfloat16
+I32 = mybir.dt.int32
+U32 = mybir.dt.uint32
+U8 = mybir.dt.uint8
+FP8X4 = mybir.dt.float8_e4m3fn_x4
+FP4X4 = mybir.dt.float4_e2m1fn_x4
+
+P = 128
+TOKENS = 8192
+K = 512
+RANK = 128
+D_OUT = 128
+TILES = TOKENS // P
+GROUP = 4
+GROUPS = TILES // GROUP
+HALF = GROUP // 2
+HA_LOAD = 4
+WORDS = K // 2
+
+FLOPS = 2 * TOKENS * (K + RANK) * D_OUT
+
+
+def tile_loramlp_pb_t_kernel(tc, h, ha, W_down_words, W_down_scales, B_down, out):
+    nc = tc.nc
+    h_rows = h.rearrange("(p j) k -> p j k", j=TILES)
+    ha_rows = ha.rearrange("(p j) r -> p j r", j=TILES)
+    out_rows = out.rearrange("(p j) d -> p j d", j=TILES)
+
+    with ExitStack() as ctx:
+        resident = ctx.enter_context(tc.tile_pool(name="resident", bufs=1))
+        stage = ctx.enter_context(tc.tile_pool(name="stage", bufs=3))
+        psum = ctx.enter_context(tc.psum_pool(name="psum", bufs=1))
+        ctx.enter_context(tc.manual_schedule())
+
+        ident_f32 = resident.tile([P, P], F32, name="ident_f32")
+        make_identity(nc, ident_f32[:])
+        ident_bf16 = resident.tile([P, P], BF16, name="ident_bf16")
+        make_identity(nc, ident_bf16[:])
+
+        w_scales = resident.tile([P, D_OUT], U8, name="w_scales", align_bytes=64)
+        nc.vector.memset(w_scales[:].bitcast(I32), 0)
+        w_words = resident.tile([P, 2 * D_OUT], U8, name="w_words", align_bytes=64)
+        b_sb = resident.tile([P, D_OUT], BF16, name="b_sb")
+        nc.scalar.dma_start(out=b_sb[:], in_=B_down)
+
+        h_sb = []
+        ha_sb = []
+        for g in range(GROUPS):
+            h_tile = resident.tile([P, GROUP, K], BF16, name="h_sb%d" % g)
+            nc.sync.dma_start(out=h_tile[:], in_=h_rows[:, g * GROUP : (g + 1) * GROUP, :])
+            h_sb.append(h_tile)
+            if g % HA_LOAD == 0:
+                ha_tile = resident.tile([P, HA_LOAD * GROUP, RANK], BF16, name="ha_sb%d" % g)
+                nc.sync.dma_start(
+                    out=ha_tile[:], in_=ha_rows[:, g * GROUP : (g + HA_LOAD) * GROUP, :]
+                )
+                ha_sb.append(ha_tile)
+            if g == 0:
+                nc.sync.dma_start(
+                    out=w_words[:].bitcast(I32),
+                    in_=W_down_words.rearrange("g p b -> (g p) b").bitcast(I32),
+                )
+                scale_rows = W_down_scales.rearrange("g q n -> (g q) n").bitcast(I32)
+                for quadrant in range(4):
+                    nc.sync.dma_start(
+                        out=w_scales[32 * quadrant : 32 * quadrant + 4, :].bitcast(I32),
+                        in_=scale_rows[4 * quadrant : 4 * quadrant + 4, :],
+                    )
+
+        grouped = {}
+        haT_sb = {}
+        codes = {}
+        h_scales = {}
+        result = {}
+
+        def transpose_group(g):
+            grouped[g] = stage.tile([P, GROUP * K], BF16, name="grouped", align_bytes=64)
+            grouped_words = grouped[g][:].bitcast(F32)
+            h_words = h_sb[g][:].bitcast(F32)
+            for half in range(GROUP // HALF):
+                hT_ps = psum.tile([P, HALF, 2, P], F32, name="hT_ps", bufs=4)
+                for a in range(HALF):
+                    for u in range(2):
+                        nc.tensor.transpose(
+                            hT_ps[:, a, u, :], h_words[:, half * HALF + a, u:WORDS:2], ident_f32[:]
+                        )
+                nc.scalar.copy(
+                    out=grouped_words[:, half * HALF * WORDS : (half + 1) * HALF * WORDS].rearrange(
+                        "p (a r u) -> p a r u", a=HALF, u=2
+                    ),
+                    in_=hT_ps[:].rearrange("p a u r -> p a r u"),
+                )
+            haT_ps = psum.tile([P, GROUP, P], BF16, name="haT_ps", bufs=2)
+            first = (g % HA_LOAD) * GROUP
+            for a in range(GROUP):
+                nc.tensor.transpose(
+                    haT_ps[:, a, :], ha_sb[g // HA_LOAD][:, first + a, :], ident_bf16[:]
+                )
+            haT_sb[g] = stage.tile([P, GROUP, P], BF16, name="haT_sb")
+            nc.scalar.copy(out=haT_sb[g][:], in_=haT_ps[:])
+
+        def lora_and_quantise_group(g):
+            lora_ps = psum.tile([P, GROUP, D_OUT], F32, name="lora_ps")
+            for a in range(GROUP):
+                nc.tensor.matmul(
+                    out=lora_ps[:, a, :], lhsT=haT_sb[g][:, a, :], rhs=b_sb[:], start=True, stop=True
+                )
+            codes[g] = stage.tile([P, GROUP * P], U32, name="codes", align_bytes=64)
+            h_scales[g] = stage.tile([P, GROUP * P], U8, name="h_scales", align_bytes=64)
+            nc.vector.quantize_mx(
+                out=codes[g][:].bitcast(FP8X4), scales=h_scales[g][:], in_=grouped[g][:]
+            )
+            result[g] = resident.tile([P, GROUP, D_OUT], F32, name="result%d" % g)
+            if g % 2 == 0:
+                nc.vector.tensor_copy(out=result[g][:], in_=lora_ps[:])
+            else:
+                nc.scalar.copy(out=result[g][:], in_=lora_ps[:])
+
+        def mx_group(g):
+            mx_ps = psum.tile([P, GROUP, D_OUT], F32, name="mx_ps")
+            for a in range(GROUP):
+                tokens = slice(a * P, (a + 1) * P)
+                nc.tensor.matmul_mx(
+                    out=mx_ps[:, a, :],
+                    lhsT=codes[g][:, tokens].bitcast(FP8X4),
+                    lhsT_scale=h_scales[g][:, tokens],
+                    rhs=w_words[:].bitcast(FP4X4),
+                    rhs_scale=w_scales[:],
+                    start=True,
+                    stop=True,
+                )
+            nc.vector.tensor_tensor(
+                out=result[g][:], in0=mx_ps[:], in1=result[g][:], op=mybir.AluOpType.add
+            )
+            nc.sync.dma_start(out=out_rows[:, g * GROUP : (g + 1) * GROUP, :], in_=result[g][:])
+
+        for i in range(GROUPS + 2):
+            if i < GROUPS:
+                transpose_group(i)
+            if 1 <= i <= GROUPS:
+                lora_and_quantise_group(i - 1)
+            if i >= 2:
+                mx_group(i - 2)

@@ -73,11 +73,19 @@ def tile_loramlp_pb_t_kernel(tc, h, ha, W_down_words, W_down_scales, B_down, out
                         in_=scale_rows[4 * quadrant : 4 * quadrant + 4, :],
                     )
 
+        packed = {}
         grouped = {}
         haT_sb = {}
         codes = {}
         h_scales = {}
         result = {}
+
+        def pack_words(g):
+            packed[g] = stage.tile([P, GROUP // 2, 2, P], F32, name="packed")
+            nc.vector.tensor_copy(
+                out=packed[g][:],
+                in_=h_sb[g][:].bitcast(F32)[:, 1:GROUP:2, :].rearrange("p a (w u) -> p a u w", u=2),
+            )
 
         def transpose_group(g):
             grouped[g] = stage.tile([P, GROUP * K], BF16, name="grouped", align_bytes=64)
@@ -85,11 +93,12 @@ def tile_loramlp_pb_t_kernel(tc, h, ha, W_down_words, W_down_scales, B_down, out
             h_words = h_sb[g][:].bitcast(F32)
             for half in range(GROUP // HALF):
                 hT_ps = psum.tile([P, HALF, 2, P], F32, name="hT_ps", bufs=4)
-                for a in range(HALF):
-                    for u in range(2):
-                        nc.tensor.transpose(
-                            hT_ps[:, a, u, :], h_words[:, half * HALF + a, u:WORDS:2], ident_f32[:]
-                        )
+                for u in range(2):
+                    nc.tensor.transpose(
+                        hT_ps[:, 0, u, :], h_words[:, half * HALF, u:WORDS:2], ident_f32[:]
+                    )
+                for u in range(2):
+                    nc.tensor.transpose(hT_ps[:, 1, u, :], packed[g][:, half, u, :], ident_f32[:])
                 nc.scalar.copy(
                     out=grouped_words[:, half * HALF * WORDS : (half + 1) * HALF * WORDS].rearrange(
                         "p (a r u) -> p a r u", a=HALF, u=2
@@ -117,7 +126,7 @@ def tile_loramlp_pb_t_kernel(tc, h, ha, W_down_words, W_down_scales, B_down, out
                 out=codes[g][:].bitcast(FP8X4), scales=h_scales[g][:], in_=grouped[g][:]
             )
             result[g] = resident.tile([P, GROUP, D_OUT], F32, name="result%d" % g)
-            if g % 2 == 0:
+            if g % 4 == 0:
                 nc.vector.tensor_copy(out=result[g][:], in_=lora_ps[:])
             else:
                 nc.scalar.copy(out=result[g][:], in_=lora_ps[:])
@@ -140,7 +149,10 @@ def tile_loramlp_pb_t_kernel(tc, h, ha, W_down_words, W_down_scales, B_down, out
             )
             nc.sync.dma_start(out=out_rows[:, g * GROUP : (g + 1) * GROUP, :], in_=result[g][:])
 
+        pack_words(0)
         for i in range(GROUPS + 2):
+            if i + 1 < GROUPS:
+                pack_words(i + 1)
             if i < GROUPS:
                 transpose_group(i)
             if 1 <= i <= GROUPS:

@@ -53,7 +53,12 @@ def tile_loramlp_pb_t_kernel(tc, h, ha, W_down_words, W_down_scales, B_down, out
         ha_sb = []
         for g in range(GROUPS):
             h_tile = resident.tile([P, GROUP, K], BF16, name="h_sb%d" % g)
-            nc.sync.dma_start(out=h_tile[:], in_=h_rows[:, g * GROUP : (g + 1) * GROUP, :])
+            step = HALF if g == 0 else GROUP
+            for a in range(0, GROUP, step):
+                nc.sync.dma_start(
+                    out=h_tile[:, a : a + step, :],
+                    in_=h_rows[:, g * GROUP + a : g * GROUP + a + step, :],
+                )
             h_sb.append(h_tile)
             if g % HA_LOAD == 0:
                 ha_tile = resident.tile([P, HA_LOAD * GROUP, RANK], BF16, name="ha_sb%d" % g)
@@ -61,7 +66,7 @@ def tile_loramlp_pb_t_kernel(tc, h, ha, W_down_words, W_down_scales, B_down, out
                     out=ha_tile[:], in_=ha_rows[:, g * GROUP : (g + HA_LOAD) * GROUP, :]
                 )
                 ha_sb.append(ha_tile)
-            if g == 0:
+            if g == 1:
                 nc.sync.dma_start(
                     out=w_words[:].bitcast(I32),
                     in_=W_down_words.rearrange("g p b -> (g p) b").bitcast(I32),
@@ -81,10 +86,10 @@ def tile_loramlp_pb_t_kernel(tc, h, ha, W_down_words, W_down_scales, B_down, out
         result = {}
 
         def pack_words(g):
-            packed[g] = stage.tile([P, GROUP // 2, 2, P], F32, name="packed")
+            packed[g] = stage.tile([P, HALF, 2, P], F32, name="packed")
             nc.vector.tensor_copy(
                 out=packed[g][:],
-                in_=h_sb[g][:].bitcast(F32)[:, 1:GROUP:2, :].rearrange("p a (w u) -> p a u w", u=2),
+                in_=h_sb[g][:].bitcast(F32)[:, HALF:GROUP, :].rearrange("p a (w u) -> p a u w", u=2),
             )
 
         def transpose_group(g):
@@ -93,19 +98,20 @@ def tile_loramlp_pb_t_kernel(tc, h, ha, W_down_words, W_down_scales, B_down, out
             h_words = h_sb[g][:].bitcast(F32)
             for half in range(GROUP // HALF):
                 hT_ps = psum.tile([P, HALF, 2, P], F32, name="hT_ps", bufs=4)
-                for u in range(2):
-                    nc.tensor.transpose(
-                        hT_ps[:, 0, u, :], h_words[:, half * HALF, u:WORDS:2], ident_f32[:]
-                    )
-                for u in range(2):
-                    nc.tensor.transpose(hT_ps[:, 1, u, :], packed[g][:, half, u, :], ident_f32[:])
+                for a in range(HALF):
+                    for u in range(2):
+                        if half == 0:
+                            words = h_words[:, a, u:WORDS:2]
+                        else:
+                            words = packed[g][:, a, u, :]
+                        nc.tensor.transpose(hT_ps[:, a, u, :], words, ident_f32[:])
                 nc.scalar.copy(
                     out=grouped_words[:, half * HALF * WORDS : (half + 1) * HALF * WORDS].rearrange(
                         "p (a r u) -> p a r u", a=HALF, u=2
                     ),
                     in_=hT_ps[:].rearrange("p a u r -> p a r u"),
                 )
-            haT_ps = psum.tile([P, GROUP, P], BF16, name="haT_ps", bufs=2)
+            haT_ps = psum.tile([P, GROUP, P], BF16, name="haT_ps")
             first = (g % HA_LOAD) * GROUP
             for a in range(GROUP):
                 nc.tensor.transpose(
@@ -126,13 +132,13 @@ def tile_loramlp_pb_t_kernel(tc, h, ha, W_down_words, W_down_scales, B_down, out
                 out=codes[g][:].bitcast(FP8X4), scales=h_scales[g][:], in_=grouped[g][:]
             )
             result[g] = resident.tile([P, GROUP, D_OUT], F32, name="result%d" % g)
-            if g % 4 == 0:
+            if g % 2 == 0:
                 nc.vector.tensor_copy(out=result[g][:], in_=lora_ps[:])
             else:
                 nc.scalar.copy(out=result[g][:], in_=lora_ps[:])
 
         def mx_group(g):
-            mx_ps = psum.tile([P, GROUP, D_OUT], F32, name="mx_ps")
+            mx_ps = psum.tile([P, GROUP, D_OUT], F32, name="mx_ps", bufs=2)
             for a in range(GROUP):
                 tokens = slice(a * P, (a + 1) * P)
                 nc.tensor.matmul_mx(

@@ -84,6 +84,7 @@ def tile_loramlp_pb_t_kernel(tc, h, ha, W_down_words, W_down_scales, B_down, out
         codes = {}
         h_scales = {}
         result = {}
+        haT_bank = {}
 
         def pack_words(g):
             packed[g] = stage.tile([P, HALF, 2, P], F32, name="packed")
@@ -117,8 +118,11 @@ def tile_loramlp_pb_t_kernel(tc, h, ha, W_down_words, W_down_scales, B_down, out
                 nc.tensor.transpose(
                     haT_ps[:, a, :], ha_sb[g // HA_LOAD][:, first + a, :], ident_bf16[:]
                 )
+            haT_bank[g] = haT_ps
+
+        def ha_out_group(g):
             haT_sb[g] = stage.tile([P, GROUP, P], BF16, name="haT_sb")
-            nc.scalar.copy(out=haT_sb[g][:], in_=haT_ps[:])
+            nc.vector.tensor_copy(out=haT_sb[g][:], in_=haT_bank[g][:])
 
         def lora_and_quantise_group(g):
             lora_ps = psum.tile([P, GROUP, D_OUT], F32, name="lora_ps")
@@ -132,10 +136,7 @@ def tile_loramlp_pb_t_kernel(tc, h, ha, W_down_words, W_down_scales, B_down, out
                 out=codes[g][:].bitcast(FP8X4), scales=h_scales[g][:], in_=grouped[g][:]
             )
             result[g] = resident.tile([P, GROUP, D_OUT], F32, name="result%d" % g)
-            if g % 2 == 0:
-                nc.vector.tensor_copy(out=result[g][:], in_=lora_ps[:])
-            else:
-                nc.scalar.copy(out=result[g][:], in_=lora_ps[:])
+            nc.scalar.copy(out=result[g][:], in_=lora_ps[:])
 
         def mx_group(g):
             mx_ps = psum.tile([P, GROUP, D_OUT], F32, name="mx_ps", bufs=2)
@@ -163,5 +164,7 @@ def tile_loramlp_pb_t_kernel(tc, h, ha, W_down_words, W_down_scales, B_down, out
                 transpose_group(i)
             if 1 <= i <= GROUPS:
                 lora_and_quantise_group(i - 1)
+            if i < GROUPS:
+                ha_out_group(i)
             if i >= 2:
                 mx_group(i - 2)

@@ -22,6 +22,7 @@ GROUPS = TILES // GROUP
 HALF = GROUP // 2
 HA_LOAD = 4
 WORDS = K // 2
+HOLD = 8
 
 FLOPS = 2 * TOKENS * (K + RANK) * D_OUT
 
@@ -53,19 +54,19 @@ def tile_loramlp_pb_t_kernel(tc, h, ha, W_down_words, W_down_scales, B_down, out
         ha_sb = []
         for g in range(GROUPS):
             h_tile = resident.tile([P, GROUP, K], BF16, name="h_sb%d" % g)
-            step = HALF if g == 0 else GROUP
-            for a in range(0, GROUP, step):
+            if g % HA_LOAD == 0:
+                ha_tile = resident.tile([P, HA_LOAD * GROUP, RANK], BF16, name="ha_sb%d" % g)
+                ha_sb.append(ha_tile)
+            cuts = (0, HALF, GROUP) if g == 0 else (0, GROUP)
+            for a, b in zip(cuts[:-1], cuts[1:]):
                 nc.sync.dma_start(
-                    out=h_tile[:, a : a + step, :],
-                    in_=h_rows[:, g * GROUP + a : g * GROUP + a + step, :],
+                    out=h_tile[:, a:b, :], in_=h_rows[:, g * GROUP + a : g * GROUP + b, :]
                 )
             h_sb.append(h_tile)
             if g % HA_LOAD == 0:
-                ha_tile = resident.tile([P, HA_LOAD * GROUP, RANK], BF16, name="ha_sb%d" % g)
                 nc.sync.dma_start(
                     out=ha_tile[:], in_=ha_rows[:, g * GROUP : (g + HA_LOAD) * GROUP, :]
                 )
-                ha_sb.append(ha_tile)
             if g == 1:
                 nc.sync.dma_start(
                     out=w_words[:].bitcast(I32),
@@ -80,11 +81,13 @@ def tile_loramlp_pb_t_kernel(tc, h, ha, W_down_words, W_down_scales, B_down, out
 
         packed = {}
         grouped = {}
+        haT_bank = {}
         haT_sb = {}
+        lora_bank = {}
         codes = {}
         h_scales = {}
+        mx_bank = {}
         result = {}
-        haT_bank = {}
 
         def pack_words(g):
             packed[g] = stage.tile([P, HALF, 2, P], F32, name="packed")
@@ -93,7 +96,7 @@ def tile_loramlp_pb_t_kernel(tc, h, ha, W_down_words, W_down_scales, B_down, out
                 in_=h_sb[g][:].bitcast(F32)[:, HALF:GROUP, :].rearrange("p a (w u) -> p a u w", u=2),
             )
 
-        def transpose_group(g):
+        def transpose_h(g):
             grouped[g] = stage.tile([P, GROUP * K], BF16, name="grouped", align_bytes=64)
             grouped_words = grouped[g][:].bitcast(F32)
             h_words = h_sb[g][:].bitcast(F32)
@@ -112,38 +115,48 @@ def tile_loramlp_pb_t_kernel(tc, h, ha, W_down_words, W_down_scales, B_down, out
                     ),
                     in_=hT_ps[:].rearrange("p a u r -> p a r u"),
                 )
-            haT_ps = psum.tile([P, GROUP, P], BF16, name="haT_ps")
+
+        def transpose_ha(g):
+            haT_bank[g] = psum.tile([P, GROUP, P], BF16, name="haT_ps")
             first = (g % HA_LOAD) * GROUP
             for a in range(GROUP):
                 nc.tensor.transpose(
-                    haT_ps[:, a, :], ha_sb[g // HA_LOAD][:, first + a, :], ident_bf16[:]
+                    haT_bank[g][:, a, :], ha_sb[g // HA_LOAD][:, first + a, :], ident_bf16[:]
                 )
-            haT_bank[g] = haT_ps
 
-        def ha_out_group(g):
+        def ha_out(g):
             haT_sb[g] = stage.tile([P, GROUP, P], BF16, name="haT_sb")
             nc.vector.tensor_copy(out=haT_sb[g][:], in_=haT_bank[g][:])
 
-        def lora_and_quantise_group(g):
-            lora_ps = psum.tile([P, GROUP, D_OUT], F32, name="lora_ps")
-            for a in range(GROUP):
+        def lora(g, tiles):
+            if g not in lora_bank:
+                lora_bank[g] = psum.tile([P, GROUP, D_OUT], F32, name="lora_ps")
+            for a in tiles:
                 nc.tensor.matmul(
-                    out=lora_ps[:, a, :], lhsT=haT_sb[g][:, a, :], rhs=b_sb[:], start=True, stop=True
+                    out=lora_bank[g][:, a, :],
+                    lhsT=haT_sb[g][:, a, :],
+                    rhs=b_sb[:],
+                    start=True,
+                    stop=True,
                 )
+
+        def lora_out(g):
+            result[g] = resident.tile([P, GROUP, D_OUT], F32, name="result%d" % g)
+            nc.scalar.copy(out=result[g][:], in_=lora_bank[g][:])
+
+        def quantise(g):
             codes[g] = stage.tile([P, GROUP * P], U32, name="codes", align_bytes=64)
             h_scales[g] = stage.tile([P, GROUP * P], U8, name="h_scales", align_bytes=64)
             nc.vector.quantize_mx(
                 out=codes[g][:].bitcast(FP8X4), scales=h_scales[g][:], in_=grouped[g][:]
             )
-            result[g] = resident.tile([P, GROUP, D_OUT], F32, name="result%d" % g)
-            nc.scalar.copy(out=result[g][:], in_=lora_ps[:])
 
-        def mx_group(g):
-            mx_ps = psum.tile([P, GROUP, D_OUT], F32, name="mx_ps", bufs=2)
+        def mx(g):
+            mx_bank[g] = psum.tile([P, GROUP, D_OUT], F32, name="mx_ps", bufs=2)
             for a in range(GROUP):
                 tokens = slice(a * P, (a + 1) * P)
                 nc.tensor.matmul_mx(
-                    out=mx_ps[:, a, :],
+                    out=mx_bank[g][:, a, :],
                     lhsT=codes[g][:, tokens].bitcast(FP8X4),
                     lhsT_scale=h_scales[g][:, tokens],
                     rhs=w_words[:].bitcast(FP4X4),
@@ -151,20 +164,35 @@ def tile_loramlp_pb_t_kernel(tc, h, ha, W_down_words, W_down_scales, B_down, out
                     start=True,
                     stop=True,
                 )
-            nc.vector.tensor_tensor(
-                out=result[g][:], in0=mx_ps[:], in1=result[g][:], op=mybir.AluOpType.add
-            )
+
+        def store(g):
             nc.sync.dma_start(out=out_rows[:, g * GROUP : (g + 1) * GROUP, :], in_=result[g][:])
 
+        def add_and_store(g):
+            nc.vector.tensor_tensor(
+                out=result[g][:], in0=mx_bank[g][:], in1=result[g][:], op=mybir.AluOpType.add
+            )
+            if g == HOLD:
+                store(g)
+                for earlier in range(HOLD):
+                    store(earlier)
+            elif g > HOLD:
+                store(g)
+
+        whole = range(GROUP)
         pack_words(0)
         for i in range(GROUPS + 2):
             if i + 1 < GROUPS:
                 pack_words(i + 1)
             if i < GROUPS:
-                transpose_group(i)
+                transpose_h(i)
+                transpose_ha(i)
             if 1 <= i <= GROUPS:
-                lora_and_quantise_group(i - 1)
+                lora(i - 1, whole)
+                quantise(i - 1)
+                lora_out(i - 1)
             if i < GROUPS:
-                ha_out_group(i)
+                ha_out(i)
             if i >= 2:
-                mx_group(i - 2)
+                mx(i - 2)
+                add_and_store(i - 2)

from contextlib import ExitStack

import concourse.mybir as mybir
from concourse.masks import make_identity

F32 = mybir.dt.float32
BF16 = mybir.dt.bfloat16
I32 = mybir.dt.int32
U32 = mybir.dt.uint32
U8 = mybir.dt.uint8
FP8X4 = mybir.dt.float8_e4m3fn_x4
FP4X4 = mybir.dt.float4_e2m1fn_x4

P = 128
TOKENS = 8192
K = 512
RANK = 128
D_OUT = 128
TILES = TOKENS // P
GROUP = 4
GROUPS = TILES // GROUP
HALF = GROUP // 2
HA_LOAD = 4
WORDS = K // 2
HOLD = 8

FLOPS = 2 * TOKENS * (K + RANK) * D_OUT


def tile_loramlp_pb_t_kernel(tc, h, ha, W_down_words, W_down_scales, B_down, out):
    nc = tc.nc
    h_rows = h.rearrange("(p j) k -> p j k", j=TILES)
    ha_rows = ha.rearrange("(p j) r -> p j r", j=TILES)
    out_rows = out.rearrange("(p j) d -> p j d", j=TILES)

    with ExitStack() as ctx:
        resident = ctx.enter_context(tc.tile_pool(name="resident", bufs=1))
        stage = ctx.enter_context(tc.tile_pool(name="stage", bufs=3))
        psum = ctx.enter_context(tc.psum_pool(name="psum", bufs=1))
        ctx.enter_context(tc.manual_schedule())

        ident_f32 = resident.tile([P, P], F32, name="ident_f32")
        make_identity(nc, ident_f32[:])
        ident_bf16 = resident.tile([P, P], BF16, name="ident_bf16")
        make_identity(nc, ident_bf16[:])

        w_scales = resident.tile([P, D_OUT], U8, name="w_scales", align_bytes=64)
        nc.vector.memset(w_scales[:].bitcast(I32), 0)
        w_words = resident.tile([P, 2 * D_OUT], U8, name="w_words", align_bytes=64)
        b_sb = resident.tile([P, D_OUT], BF16, name="b_sb")
        nc.scalar.dma_start(out=b_sb[:], in_=B_down)

        h_sb = []
        ha_sb = []
        for g in range(GROUPS):
            h_tile = resident.tile([P, GROUP, K], BF16, name="h_sb%d" % g)
            if g % HA_LOAD == 0:
                ha_tile = resident.tile([P, HA_LOAD * GROUP, RANK], BF16, name="ha_sb%d" % g)
                ha_sb.append(ha_tile)
            cuts = (0, HALF, GROUP) if g == 0 else (0, GROUP)
            for a, b in zip(cuts[:-1], cuts[1:]):
                nc.sync.dma_start(
                    out=h_tile[:, a:b, :], in_=h_rows[:, g * GROUP + a : g * GROUP + b, :]
                )
            h_sb.append(h_tile)
            if g % HA_LOAD == 0:
                nc.sync.dma_start(
                    out=ha_tile[:], in_=ha_rows[:, g * GROUP : (g + HA_LOAD) * GROUP, :]
                )
            if g == 1:
                nc.sync.dma_start(
                    out=w_words[:].bitcast(I32),
                    in_=W_down_words.rearrange("g p b -> (g p) b").bitcast(I32),
                )
                scale_rows = W_down_scales.rearrange("g q n -> (g q) n").bitcast(I32)
                for quadrant in range(4):
                    nc.sync.dma_start(
                        out=w_scales[32 * quadrant : 32 * quadrant + 4, :].bitcast(I32),
                        in_=scale_rows[4 * quadrant : 4 * quadrant + 4, :],
                    )

        packed = {}
        grouped = {}
        haT_bank = {}
        haT_sb = {}
        lora_bank = {}
        codes = {}
        h_scales = {}
        mx_bank = {}
        result = {}

        def pack_words(g):
            packed[g] = stage.tile([P, HALF, 2, P], F32, name="packed")
            nc.vector.tensor_copy(
                out=packed[g][:],
                in_=h_sb[g][:].bitcast(F32)[:, HALF:GROUP, :].rearrange("p a (w u) -> p a u w", u=2),
            )

        def transpose_h(g):
            grouped[g] = stage.tile([P, GROUP * K], BF16, name="grouped", align_bytes=64)
            grouped_words = grouped[g][:].bitcast(F32)
            h_words = h_sb[g][:].bitcast(F32)
            for half in range(GROUP // HALF):
                hT_ps = psum.tile([P, HALF, 2, P], F32, name="hT_ps", bufs=4)
                for a in range(HALF):
                    for u in range(2):
                        if half == 0:
                            words = h_words[:, a, u:WORDS:2]
                        else:
                            words = packed[g][:, a, u, :]
                        nc.tensor.transpose(hT_ps[:, a, u, :], words, ident_f32[:])
                nc.scalar.copy(
                    out=grouped_words[:, half * HALF * WORDS : (half + 1) * HALF * WORDS].rearrange(
                        "p (a r u) -> p a r u", a=HALF, u=2
                    ),
                    in_=hT_ps[:].rearrange("p a u r -> p a r u"),
                )

        def transpose_ha(g):
            haT_bank[g] = psum.tile([P, GROUP, P], BF16, name="haT_ps")
            first = (g % HA_LOAD) * GROUP
            for a in range(GROUP):
                nc.tensor.transpose(
                    haT_bank[g][:, a, :], ha_sb[g // HA_LOAD][:, first + a, :], ident_bf16[:]
                )

        def ha_out(g):
            haT_sb[g] = stage.tile([P, GROUP, P], BF16, name="haT_sb")
            nc.vector.tensor_copy(out=haT_sb[g][:], in_=haT_bank[g][:])

        def lora(g, tiles):
            if g not in lora_bank:
                lora_bank[g] = psum.tile([P, GROUP, D_OUT], F32, name="lora_ps")
            for a in tiles:
                nc.tensor.matmul(
                    out=lora_bank[g][:, a, :],
                    lhsT=haT_sb[g][:, a, :],
                    rhs=b_sb[:],
                    start=True,
                    stop=True,
                )

        def lora_out(g):
            result[g] = resident.tile([P, GROUP, D_OUT], F32, name="result%d" % g)
            nc.scalar.copy(out=result[g][:], in_=lora_bank[g][:])

        def quantise(g):
            codes[g] = stage.tile([P, GROUP * P], U32, name="codes", align_bytes=64)
            h_scales[g] = stage.tile([P, GROUP * P], U8, name="h_scales", align_bytes=64)
            nc.vector.quantize_mx(
                out=codes[g][:].bitcast(FP8X4), scales=h_scales[g][:], in_=grouped[g][:]
            )

        def mx(g):
            mx_bank[g] = psum.tile([P, GROUP, D_OUT], F32, name="mx_ps", bufs=2)
            for a in range(GROUP):
                tokens = slice(a * P, (a + 1) * P)
                nc.tensor.matmul_mx(
                    out=mx_bank[g][:, a, :],
                    lhsT=codes[g][:, tokens].bitcast(FP8X4),
                    lhsT_scale=h_scales[g][:, tokens],
                    rhs=w_words[:].bitcast(FP4X4),
                    rhs_scale=w_scales[:],
                    start=True,
                    stop=True,
                )

        def store(g):
            nc.sync.dma_start(out=out_rows[:, g * GROUP : (g + 1) * GROUP, :], in_=result[g][:])

        def add_and_store(g):
            nc.vector.tensor_tensor(
                out=result[g][:], in0=mx_bank[g][:], in1=result[g][:], op=mybir.AluOpType.add
            )
            if g == HOLD:
                store(g)
                for earlier in range(HOLD):
                    store(earlier)
            elif g > HOLD:
                store(g)

        whole = range(GROUP)
        pack_words(0)
        for i in range(GROUPS + 2):
            if i + 1 < GROUPS:
                pack_words(i + 1)
            if i < GROUPS:
                transpose_h(i)
                transpose_ha(i)
            if 1 <= i <= GROUPS:
                lora(i - 1, whole)
                quantise(i - 1)
                lora_out(i - 1)
            if i < GROUPS:
                ha_out(i)
            if i >= 2:
                mx(i - 2)
                add_and_store(i - 2)
